import numpy as np
import ml_dtypes


def mxq(x, axis, fmt="e4m3"):
    dtype, down = {"e4m3": (ml_dtypes.float8_e4m3fn, 7), "e5m2": (ml_dtypes.float8_e5m2, 14)}[fmt]
    v = np.moveaxis(np.asarray(x, np.float32).astype(ml_dtypes.bfloat16).astype(np.float64), axis, -1)
    blocks = v.reshape(v.shape[:-1] + (-1, 32))
    amax = np.abs(blocks).max(-1, keepdims=True)
    byte = np.maximum(np.where(amax > 0, np.frexp(amax)[1] - 1 + 127, 0) - down, 1)
    scale = np.exp2(byte - 127.0)
    codes = (blocks / scale).astype(np.float32).astype(dtype).astype(np.float64)
    return np.moveaxis((codes * scale).reshape(v.shape), -1, axis)


WIDE = False


def mx_kscale(k):
    if not WIDE:
        return np.ones(k)
    levels = np.array([10, -10, 5, -5, 0])
    if k % 512:
        return np.exp2(np.random.permutation(np.resize(levels, k // 32))).repeat(32)
    a = np.empty((k // 512, 16))
    for p in range(k // 512):
        a[p, :8] = np.random.permutation(np.resize(levels, 8))
        for g in range(8):
            far = levels[np.abs(levels - a[p, g]) >= 10]
            a[p, g + 8] = far[np.random.randint(len(far))]
    return np.exp2(a.ravel()).repeat(32)


BF16 = ml_dtypes.bfloat16


def bf(x):
    return np.asarray(x, np.float32).astype(BF16)


def f64(x):
    return np.asarray(x).astype(np.float64)


N, T, D, B0, C, P0, V1, P1, V2 = 2, 512, 1024, 2046, 2, 512, 2048, 512, 1024
MU = 0.25
SIG = 2.0


def softmax(v):
    e = np.exp(v - v.max(-1, keepdims=True))
    return e / e.sum(-1, keepdims=True)


def setup_inputs():
    s, t = mx_kscale(D), mx_kscale(P0)
    hw = np.random.standard_normal((D, B0 + C)) * SIG / np.sqrt(D)
    hw[:, B0:] = hw[:, B0:] / SIG + (np.log(B0) + 0.5 * SIG * SIG) / (MU * D)
    return {"x": bf((np.random.standard_normal((N, T, D)) + MU) * s),
            "head_weight": bf(hw / s[:, None]),
            "tail_proj_0": bf(np.random.standard_normal((D, P0)) / np.sqrt(D) / s[:, None] * t),
            "tail_w_0": bf(np.random.standard_normal((P0, V1)) * SIG / np.sqrt(P0) / t[:, None])}


def reference(x, head_weight, tail_proj_0, tail_w_0):
    xq = mxq(f64(x), 2, "e4m3")
    head_sm = softmax(xq @ mxq(f64(head_weight), 0, "e4m3"))
    h = xq @ mxq(f64(tail_proj_0), 0, "e4m3")
    tail_sm = softmax(mxq(h, 2, "e4m3") @ mxq(f64(tail_w_0), 0, "e4m3"))
    probs = np.concatenate([head_sm[..., :B0], tail_sm * head_sm[..., B0:B0 + 1]], axis=-1)
    return probs, head_sm[..., B0 + 1:B0 + C]

@@ -1,0 +1,339 @@
+from contextlib import ExitStack
+
+import concourse.mybir as mybir
+from concourse.masks import make_identity
+
+F32 = mybir.dt.float32
+BF16 = mybir.dt.bfloat16
+U32 = mybir.dt.uint32
+U8 = mybir.dt.uint8
+FP8X4 = mybir.dt.float8_e4m3fn_x4
+ALU = mybir.AluOpType
+ACT = mybir.ActivationFunctionType
+AX = mybir.AxisListType
+
+P = 128
+TOKENS = 1024
+D = 1024
+V = 2048
+P0 = 512
+NT = TOKENS // P
+HEAD_TOKENS = 2046
+BANK = 512
+LAST_SPLIT = 1344
+BIG_BUFS = 13
+
+FLOPS = 2 * TOKENS * (D * V + D * P0 + P0 * V)
+
+
+def tile_adaptiveinputsoftmax_pa_kernel(tc, x, head_weight, tail_proj_0, tail_w_0, out_0, out_1):
+    nc = tc.nc
+    xf = x.flatten_outer_dims()
+    o0 = out_0.flatten_outer_dims()
+    o1 = out_1.flatten_outer_dims()
+
+    with ExitStack() as ctx:
+        ctx.enter_context(tc.manual_schedule())
+        keep = ctx.enter_context(tc.tile_pool(name="keep", bufs=1))
+        gwp = ctx.enter_context(tc.tile_pool(name="gwp", bufs=5))
+        big = ctx.enter_context(tc.tile_pool(name="big", bufs=BIG_BUFS))
+        stats = ctx.enter_context(tc.tile_pool(name="stats", bufs=4))
+        psum = ctx.enter_context(tc.psum_pool(name="psum", bufs=8))
+
+        tp_raw = big.tile([P, 2, 4, P0], BF16, tag="big", name="tp_raw")
+        for g in range(2):
+            nc.sync.dma_start(
+                out=tp_raw[:, g, :, :],
+                in_=tail_proj_0[512 * g : 512 * g + 512, :].rearrange("(p j) c -> p j c", j=4),
+            )
+        hw_raw = {}
+        for g in range(2):
+            for hf in range(2):
+                hw_part = big.tile([P, 4, 1024], BF16, tag="big", name="hw_part")
+                hw_raw[(g, hf)] = hw_part
+                nc.sync.dma_start(
+                    out=hw_part[:],
+                    in_=head_weight[512 * g : 512 * g + 512, 1024 * hf : 1024 * hf + 1024].rearrange(
+                        "(p j) c -> p j c", j=4
+                    ),
+                )
+        x_raw = {}
+        for b in range(2):
+            x_part = big.tile([P, 4, D], BF16, tag="big", name="x_part")
+            x_raw[b] = x_part
+            for a in range(2):
+                t0 = 512 * b + 256 * a
+                nc.sync.dma_start(
+                    out=x_part[:, 2 * a : 2 * a + 2, :],
+                    in_=xf[t0 : t0 + 256, :].rearrange("(i p) k -> p i k", p=P),
+                )
+        tw_raw = {}
+        for hf in range(2):
+            tw_part = big.tile([P, 4, 1024], BF16, tag="big", name="tw_part")
+            tw_raw[hf] = tw_part
+            nc.sync.dma_start(
+                out=tw_part[:],
+                in_=tail_w_0[:, 1024 * hf : 1024 * hf + 1024].rearrange("(p j) n -> p j n", j=4),
+            )
+
+        warm_in = keep.tile([P, 1], F32)
+        warm_out = keep.tile([P, 1], F32)
+        nc.vector.memset(warm_in[:], 0.0)
+        nc.scalar.activation(out=warm_out[:], in_=warm_in[:], func=ACT.Exp)
+        cl = keep.tile([P, 2, P], F32)
+        nc.vector.memset(cl[:], 0.0)
+        ident = keep.tile([P, P], F32)
+        make_identity(nc, ident[:])
+
+        x_codes = keep.tile([P, NT, 2 * P], U32, align_bytes=64)
+        x_scales = keep.tile([P, NT, 2 * P], U8, align_bytes=64)
+        tp_codes = keep.tile([P, 2, P0], U32, align_bytes=64)
+        tp_scales = keep.tile([P, 2, P0], U8, align_bytes=64)
+        hw_codes = keep.tile([P, 2, V], U32, align_bytes=64)
+        hw_scales = keep.tile([P, 2, V], U8, align_bytes=64)
+        tw_codes = keep.tile([P, V], U32, align_bytes=64)
+        tw_scales = keep.tile([P, V], U8, align_bytes=64)
+        gx = keep.tile([P, NT, 2, P, 2], F32, align_bytes=64)
+        gh = keep.tile([P, NT, P, 4], BF16, align_bytes=64)
+        h_codes = keep.tile([P, NT * P], U32, align_bytes=64)
+        h_scales = keep.tile([P, NT * P], U8, align_bytes=64)
+
+        units = {}
+        for g in range(2):
+            units["A%d" % g] = (tp_raw[:, g, :, :], tp_codes[:, g, :], tp_scales[:, g, :])
+        for n in range(8):
+            g, c = divmod(n, 4)
+            cols = slice(BANK * c, BANK * c + BANK)
+            part = slice(BANK * (c % 2), BANK * (c % 2) + BANK)
+            units["B%d" % n] = (hw_raw[(g, c // 2)][:, :, part], hw_codes[:, g, cols], hw_scales[:, g, cols])
+        for c in range(4):
+            cols = slice(BANK * c, BANK * c + BANK)
+            part = slice(BANK * (c % 2), BANK * (c % 2) + BANK)
+            units["C%d" % c] = (tw_raw[c // 2][:, :, part], tw_codes[:, cols], tw_scales[:, cols])
+        grouped = {}
+
+        def regroup(u, on_scalar):
+            gw = gwp.tile([P, BANK, 4], BF16, align_bytes=64, name="gw")
+            grouped[u] = gw
+            if u[0] == "A":
+                dst_v = gw[:].rearrange("p (t m) j -> p t m j", t=4)
+                src_v = units[u][0].rearrange("p j (m t) -> p t m j", t=4)
+            else:
+                dst_v = gw[:].rearrange("p (c i) t -> p c t i", i=4)
+                src_v = units[u][0].rearrange("p t (c i) -> p c t i", i=4)
+            if on_scalar:
+                nc.scalar.copy(out=dst_v, in_=src_v)
+            else:
+                nc.vector.tensor_copy(out=dst_v, in_=src_v)
+
+        def quantise(u):
+            nc.vector.quantize_mx(
+                out=units[u][1].bitcast(FP8X4),
+                scales=units[u][2],
+                in_=grouped[u][:].rearrange("p w t -> p (w t)"),
+            )
+
+        banks = {}
+
+        def new_bank(key):
+            bank = psum.tile([P, BANK], F32, tag="bank", name="bank")
+            banks[key] = bank
+            return bank
+
+        def x_transpose(i):
+            xw = x_raw[i // 4][:, i % 4, :].bitcast(F32)
+            bank = new_bank(("x", i))
+            for c in range(4):
+                g, u = divmod(c, 2)
+                nc.tensor.transpose(
+                    bank[:, P * c : P * c + P], xw[:, 256 * g + u : 256 * (g + 1) : 2], ident[:]
+                )
+
+        def x_out(i):
+            nc.scalar.copy(
+                out=gx[:, i, :, :, :], in_=banks[("x", i)][:].rearrange("p (g u r) -> p g r u", g=2, u=2)
+            )
+
+        def x_quantise(i):
+            nc.vector.quantize_mx(
+                out=x_codes[:, i, :].bitcast(FP8X4),
+                scales=x_scales[:, i, :],
+                in_=gx[:, i, :, :, :].rearrange("p g r u -> p (g r u)").bitcast(BF16),
+            )
+
+        def h_matmuls(i):
+            bank = new_bank(("h", i))
+            for j in range(4):
+                for g in range(2):
+                    nc.tensor.matmul_mx(
+                        out=bank[:, P * j : P * j + P],
+                        lhsT=tp_codes[:, g, P * j : P * j + P].bitcast(FP8X4),
+                        lhsT_scale=tp_scales[:, g, P * j : P * j + P],
+                        rhs=x_codes[:, i, P * g : P * g + P].bitcast(FP8X4),
+                        rhs_scale=x_scales[:, i, P * g : P * g + P],
+                        start=(g == 0),
+                        stop=(g == 1),
+                    )
+
+        def h_out(i):
+            nc.scalar.copy(out=gh[:, i, :, :], in_=banks[("h", i)][:].rearrange("p (j r) -> p r j", j=4))
+
+        def h_quantise(a):
+            nc.vector.quantize_mx(
+                out=h_codes[:, 512 * a : 512 * a + 512].bitcast(FP8X4),
+                scales=h_scales[:, 512 * a : 512 * a + 512],
+                in_=gh[:, 4 * a : 4 * a + 4, :, :].rearrange("p i r j -> p (i r j)"),
+            )
+
+        def logits(n):
+            i = n % NT
+            for c in range(4):
+                cols = slice(BANK * c, BANK * c + BANK)
+                bank = new_bank((n, c))
+                if n < NT:
+                    for g in range(2):
+                        nc.tensor.matmul_mx(
+                            out=bank[:],
+                            lhsT=x_codes[:, i, P * g : P * g + P].bitcast(FP8X4),
+                            lhsT_scale=x_scales[:, i, P * g : P * g + P],
+                            rhs=hw_codes[:, g, cols].bitcast(FP8X4),
+                            rhs_scale=hw_scales[:, g, cols],
+                            start=(g == 0),
+                            stop=(g == 1),
+                        )
+                else:
+                    nc.tensor.matmul_mx(
+                        out=bank[:],
+                        lhsT=h_codes[:, P * i : P * i + P].bitcast(FP8X4),
+                        lhsT_scale=h_scales[:, P * i : P * i + P],
+                        rhs=tw_codes[:, cols].bitcast(FP8X4),
+                        rhs_scale=tw_scales[:, cols],
+                        start=True,
+                        stop=True,
+                    )
+
+        small = {}
+
+        def row_max(n):
+            e = big.tile([P, V], F32, tag="big", name="e")
+            small[("e", n)] = e
+            m4 = stats.tile([P, 4], F32, name="m4")
+            for c in range(4):
+                nc.vector.tensor_scalar(
+                    out=e[:, BANK * c : BANK * c + BANK], in0=banks[(n, c)][:], scalar1=1.0, scalar2=None,
+                    op0=ALU.mult, op1=ALU.max, accum_out=m4[:, c : c + 1],
+                )
+            negm = stats.tile([P, 1], F32, name="negm")
+            nc.vector.tensor_reduce(out=negm[:], in_=m4[:], axis=AX.X, op=ALU.max, negate=True)
+            small[("negm", n)] = negm
+
+        def exps(n):
+            e = small[("e", n)]
+            s = stats.tile([P, 1], F32, name="s")
+            small[("s", n)] = s
+            nc.scalar.activation(
+                out=e[:], in_=e[:], func=ACT.Exp, bias=small[("negm", n)][:, 0:1], scale=1.0, accum_out=s[:]
+            )
+
+        def finish(n):
+            i = n % NT
+            rows = slice(P * i, P * i + P)
+            e = small[("e", n)]
+            s = small[("s", n)]
+            r = stats.tile([P, 1], F32, name="r")
+            nc.vector.reciprocal(out=r[:], in_=s[:])
+            if n < NT:
+                cuts = (0, 1024, HEAD_TOKENS) if n == 0 else (0, HEAD_TOKENS)
+                for lo, hi in zip(cuts[:-1], cuts[1:]):
+                    nc.gpsimd.tensor_scalar(
+                        out=e[:, lo:hi], in0=e[:, lo:hi],
+                        scalar1=r[:, 0:1], scalar2=0.0, op0=ALU.mult, op1=ALU.add,
+                    )
+                    nc.sync.dma_start(out=o0[rows, lo:hi], in_=e[:, lo:hi])
+                nc.gpsimd.tensor_scalar(
+                    out=cl[:, :, i], in0=e[:, HEAD_TOKENS:V], scalar1=r[:, 0:1], scalar2=0.0,
+                    op0=ALU.mult, op1=ALU.add,
+                )
+            elif n < 2 * NT - 2:
+                nc.gpsimd.tensor_scalar(
+                    out=e[:], in0=e[:],
+                    scalar1=r[:, 0:1], scalar2=cl[:, 0, i : i + 1], op0=ALU.mult, op1=ALU.mult,
+                )
+                nc.sync.dma_start(out=o0[rows, HEAD_TOKENS : HEAD_TOKENS + V], in_=e[:])
+            elif n == 2 * NT - 2:
+                for hf in range(2):
+                    cols = slice(1024 * hf, 1024 * hf + 1024)
+                    nc.gpsimd.tensor_scalar(
+                        out=e[:, cols], in0=e[:, cols],
+                        scalar1=r[:, 0:1], scalar2=cl[:, 0, i : i + 1], op0=ALU.mult, op1=ALU.mult,
+                    )
+                    nc.sync.dma_start(
+                        out=o0[rows, HEAD_TOKENS + 1024 * hf : HEAD_TOKENS + 1024 * hf + 1024], in_=e[:, cols]
+                    )
+            else:
+                rc = stats.tile([P, 1], F32, name="rc")
+                nc.vector.tensor_scalar(
+                    out=rc[:], in0=r[:], scalar1=cl[:, 0, i : i + 1], scalar2=None, op0=ALU.mult
+                )
+                nc.vector.tensor_scalar(
+                    out=e[:, 0:LAST_SPLIT], in0=e[:, 0:LAST_SPLIT], scalar1=rc[:, 0:1], scalar2=None, op0=ALU.mult
+                )
+                nc.scalar.activation(
+                    out=e[:, LAST_SPLIT:V], in_=e[:, LAST_SPLIT:V], func=ACT.Copy, scale=rc[:, 0:1]
+                )
+                nc.sync.dma_start(out=o0[rows, HEAD_TOKENS : HEAD_TOKENS + LAST_SPLIT], in_=e[:, 0:LAST_SPLIT])
+                nc.sync.dma_start(out=o0[rows, HEAD_TOKENS + LAST_SPLIT : HEAD_TOKENS + V], in_=e[:, LAST_SPLIT:V])
+
+        first = ["A0", "A1", "B0", "B1", "B2", "B3", "B4", "B5", "B6", "B7"]
+        for k in range(5):
+            regroup(first[2 * k + 1], True)
+            regroup(first[2 * k], False)
+            if k > 0:
+                quantise(first[2 * k - 1])
+            quantise(first[2 * k])
+        for i in range(NT):
+            x_transpose(i)
+        for i in range(NT):
+            x_out(i)
+        quantise("B7")
+        for i in range(NT):
+            x_quantise(i)
+        logits(0)
+        logits(1)
+        regroup("C1", True)
+        row_max(0)
+        regroup("C0", False)
+        quantise("C1")
+        quantise("C0")
+
+        h_tiles = {1: (0, 1), 2: (2, 3), 5: (4, 5), 6: (6, 7)}
+        late_units = {0: "C2", 3: "C3"}
+        for n in range(2 * NT):
+            if n + 2 < 2 * NT:
+                logits(n + 2)
+            exps(n)
+            if n in late_units:
+                regroup(late_units[n], True)
+            if n == 0:
+                finish(n)
+            if n + 1 < 2 * NT:
+                row_max(n + 1)
+            if n - 1 in late_units:
+                quantise(late_units[n - 1])
+            for i in h_tiles.get(n, ()):
+                h_matmuls(i)
+            for i in h_tiles.get(n, ()):
+                h_out(i)
+            if n == 9:
+                o1_bank = new_bank("o1")
+                nc.tensor.transpose(o1_bank[:, 0:P], cl[:, 1, :], ident[:])
+            if n == 3:
+                h_quantise(0)
+            if n == 7:
+                h_quantise(1)
+            if n == 9:
+                o1_sb = keep.tile([P, P], F32)
+                nc.vector.tensor_copy(out=o1_sb[:], in_=banks["o1"][:, 0:P])
+                nc.sync.dma_start(out=o1.rearrange("(i p) o -> i (p o)", p=P), in_=o1_sb[0:NT, :])
+            if n > 0:
+                finish(n)

@@ -37,7 +37,7 @@ def tile_adaptiveinputsoftmax_pa_kernel(tc, x, head_weight, tail_proj_0, tail_w_
         keep = ctx.enter_context(tc.tile_pool(name="keep", bufs=1))
         gwp = ctx.enter_context(tc.tile_pool(name="gwp", bufs=5))
         big = ctx.enter_context(tc.tile_pool(name="big", bufs=BIG_BUFS))
-        stats = ctx.enter_context(tc.tile_pool(name="stats", bufs=4))
+        stats = ctx.enter_context(tc.tile_pool(name="stats", bufs=6))
         psum = ctx.enter_context(tc.psum_pool(name="psum", bufs=8))
 
         tp_raw = big.tile([P, 2, 4, P0], BF16, tag="big", name="tp_raw")
@@ -214,17 +214,21 @@ def tile_adaptiveinputsoftmax_pa_kernel(tc, x, head_weight, tail_proj_0, tail_w_
 
         small = {}
 
-        def row_max(n):
-            e = big.tile([P, V], F32, tag="big", name="e")
-            small[("e", n)] = e
-            m4 = stats.tile([P, 4], F32, name="m4")
-            for c in range(4):
+        def row_max(n, chunks=range(4)):
+            if chunks[0] == 0:
+                small[("e", n)] = big.tile([P, V], F32, tag="big", name="e")
+                small[("m4", n)] = stats.tile([P, 4], F32, name="m4")
+            e = small[("e", n)]
+            m4 = small[("m4", n)]
+            for c in chunks:
                 nc.vector.tensor_scalar(
                     out=e[:, BANK * c : BANK * c + BANK], in0=banks[(n, c)][:], scalar1=1.0, scalar2=None,
                     op0=ALU.mult, op1=ALU.max, accum_out=m4[:, c : c + 1],
                 )
+
+        def negate_max(n):
             negm = stats.tile([P, 1], F32, name="negm")
-            nc.vector.tensor_reduce(out=negm[:], in_=m4[:], axis=AX.X, op=ALU.max, negate=True)
+            nc.vector.tensor_reduce(out=negm[:], in_=small[("m4", n)][:], axis=AX.X, op=ALU.max, negate=True)
             small[("negm", n)] = negm
 
         def exps(n):
@@ -303,6 +307,7 @@ def tile_adaptiveinputsoftmax_pa_kernel(tc, x, head_weight, tail_proj_0, tail_w_
         regroup("C1", True)
         row_max(0)
         regroup("C0", False)
+        negate_max(0)
         quantise("C1")
         quantise("C0")
 
@@ -311,13 +316,17 @@ def tile_adaptiveinputsoftmax_pa_kernel(tc, x, head_weight, tail_proj_0, tail_w_
         for n in range(2 * NT):
             if n + 2 < 2 * NT:
                 logits(n + 2)
+            if n + 1 < 2 * NT:
+                row_max(n + 1, range(1))
+            if n > 0:
+                negate_max(n)
             exps(n)
+            if n > 0:
+                finish(n - 1)
             if n in late_units:
                 regroup(late_units[n], True)
-            if n == 0:
-                finish(n)
             if n + 1 < 2 * NT:
-                row_max(n + 1)
+                row_max(n + 1, range(1, 4))
             if n - 1 in late_units:
                 quantise(late_units[n - 1])
             for i in h_tiles.get(n, ()):
@@ -331,9 +340,8 @@ def tile_adaptiveinputsoftmax_pa_kernel(tc, x, head_weight, tail_proj_0, tail_w_
                 h_quantise(0)
             if n == 7:
                 h_quantise(1)
-            if n == 9:
+            if n == 10:
                 o1_sb = keep.tile([P, P], F32)
                 nc.vector.tensor_copy(out=o1_sb[:], in_=banks["o1"][:, 0:P])
                 nc.sync.dma_start(out=o1.rearrange("(i p) o -> i (p o)", p=P), in_=o1_sb[0:NT, :])
-            if n > 0:
-                finish(n)
+        finish(2 * NT - 1)

@@ -31,6 +31,7 @@ def tile_adaptiveinputsoftmax_pa_kernel(tc, x, head_weight, tail_proj_0, tail_w_
     xf = x.flatten_outer_dims()
     o0 = out_0.flatten_outer_dims()
     o1 = out_1.flatten_outer_dims()
+    o0_rows4 = o0.rearrange("(b q i) c -> b q (i c)", q=P // 4, i=4)
 
     with ExitStack() as ctx:
         ctx.enter_context(tc.manual_schedule())
@@ -80,10 +81,15 @@ def tile_adaptiveinputsoftmax_pa_kernel(tc, x, head_weight, tail_proj_0, tail_w_
         warm_out = keep.tile([P, 1], F32)
         nc.vector.memset(warm_in[:], 0.0)
         nc.scalar.activation(out=warm_out[:], in_=warm_in[:], func=ACT.Exp)
-        cl = keep.tile([P, 2, P], F32)
-        nc.vector.memset(cl[:], 0.0)
+        head_first = keep.tile([P, NT, 6], F32)
+        head_last = keep.tile([P, 2 * NT, 8], F32)
+        nc.vector.memset(head_last[:], 0.0)
+        next_first = keep.tile([P, NT, 6], F32)
         ident = keep.tile([P, P], F32)
         make_identity(nc, ident[:])
+        shift = keep.tile([P, P], F32)
+        nc.vector.memset(shift[:], 0.0)
+        nc.vector.tensor_copy(out=shift[:, 0 : P - 1], in_=ident[:, 1:P])
 
         x_codes = keep.tile([P, NT, 2 * P], U32, align_bytes=64)
         x_scales = keep.tile([P, NT, 2 * P], U8, align_bytes=64)
@@ -216,13 +222,13 @@ def tile_adaptiveinputsoftmax_pa_kernel(tc, x, head_weight, tail_proj_0, tail_w_
 
         def row_max(n, chunks=range(4)):
             if chunks[0] == 0:
-                small[("e", n)] = big.tile([P, V], F32, tag="big", name="e")
+                small[("e", n)] = big.tile([P, V + 16], F32, tag="big", name="e")
                 small[("m4", n)] = stats.tile([P, 4], F32, name="m4")
             e = small[("e", n)]
             m4 = small[("m4", n)]
             for c in chunks:
                 nc.vector.tensor_scalar(
-                    out=e[:, BANK * c : BANK * c + BANK], in0=banks[(n, c)][:], scalar1=1.0, scalar2=None,
+                    out=e[:, 8 + BANK * c : 8 + BANK * c + BANK], in0=banks[(n, c)][:], scalar1=1.0, scalar2=None,
                     op0=ALU.mult, op1=ALU.max, accum_out=m4[:, c : c + 1],
                 )
 
@@ -236,57 +242,71 @@ def tile_adaptiveinputsoftmax_pa_kernel(tc, x, head_weight, tail_proj_0, tail_w_
             s = stats.tile([P, 1], F32, name="s")
             small[("s", n)] = s
             nc.scalar.activation(
-                out=e[:], in_=e[:], func=ACT.Exp, bias=small[("negm", n)][:, 0:1], scale=1.0, accum_out=s[:]
+                out=e[:, 8 : 8 + V], in_=e[:, 8 : 8 + V], func=ACT.Exp, bias=small[("negm", n)][:, 0:1], scale=1.0, accum_out=s[:]
             )
 
+        def store_head(e, b, lo, hi):
+            for i in range(4):
+                nc.sync.dma_start(
+                    out=o0_rows4[b, :, 4096 * i + lo : 4096 * i + hi],
+                    in_=e[i:P:4, 8 + 2 * i + lo : 8 + 2 * i + hi],
+                )
+
+        def store_tail(e, b, lo, hi):
+            for i in range(4):
+                end = min(hi, 2056 if i < 3 else 2048)
+                nc.sync.dma_start(
+                    out=o0_rows4[b, :, 4096 * i + 2040 + lo : 4096 * i + 2040 + end],
+                    in_=e[i:P:4, 2 + 2 * i + lo : 2 + 2 * i + end],
+                )
+
         def finish(n):
-            i = n % NT
-            rows = slice(P * i, P * i + P)
+            b = n % NT
             e = small[("e", n)]
             s = small[("s", n)]
             r = stats.tile([P, 1], F32, name="r")
             nc.vector.reciprocal(out=r[:], in_=s[:])
             if n < NT:
-                cuts = (0, 1024, HEAD_TOKENS) if n == 0 else (0, HEAD_TOKENS)
-                for lo, hi in zip(cuts[:-1], cuts[1:]):
+                steps = ((0, 1032, 0, 1024), (1032, 2046, 1024, 2040)) if n == 0 else ((0, 2046, 0, 2040),)
+                for c0, c1, lo, hi in steps:
                     nc.gpsimd.tensor_scalar(
-                        out=e[:, lo:hi], in0=e[:, lo:hi],
+                        out=e[:, 8 + c0 : 8 + c1], in0=e[:, 8 + c0 : 8 + c1],
                         scalar1=r[:, 0:1], scalar2=0.0, op0=ALU.mult, op1=ALU.add,
                     )
-                    nc.sync.dma_start(out=o0[rows, lo:hi], in_=e[:, lo:hi])
+                    store_head(e, b, lo, hi)
+                nc.gpsimd.tensor_copy(out=head_first[:, b, :], in_=e[:, 8:14])
+                nc.gpsimd.tensor_copy(out=head_last[:, b, 0:6], in_=e[:, 2048:2054])
                 nc.gpsimd.tensor_scalar(
-                    out=cl[:, :, i], in0=e[:, HEAD_TOKENS:V], scalar1=r[:, 0:1], scalar2=0.0,
+                    out=head_last[:, b, 6:8], in0=e[:, 2054:2056], scalar1=r[:, 0:1], scalar2=0.0,
                     op0=ALU.mult, op1=ALU.add,
                 )
-            elif n < 2 * NT - 2:
-                nc.gpsimd.tensor_scalar(
-                    out=e[:], in0=e[:],
-                    scalar1=r[:, 0:1], scalar2=cl[:, 0, i : i + 1], op0=ALU.mult, op1=ALU.mult,
-                )
-                nc.sync.dma_start(out=o0[rows, HEAD_TOKENS : HEAD_TOKENS + V], in_=e[:])
-            elif n == 2 * NT - 2:
-                for hf in range(2):
-                    cols = slice(1024 * hf, 1024 * hf + 1024)
-                    nc.gpsimd.tensor_scalar(
-                        out=e[:, cols], in0=e[:, cols],
-                        scalar1=r[:, 0:1], scalar2=cl[:, 0, i : i + 1], op0=ALU.mult, op1=ALU.mult,
-                    )
-                    nc.sync.dma_start(
-                        out=o0[rows, HEAD_TOKENS + 1024 * hf : HEAD_TOKENS + 1024 * hf + 1024], in_=e[:, cols]
-                    )
             else:
-                rc = stats.tile([P, 1], F32, name="rc")
-                nc.vector.tensor_scalar(
-                    out=rc[:], in0=r[:], scalar1=cl[:, 0, i : i + 1], scalar2=None, op0=ALU.mult
-                )
-                nc.vector.tensor_scalar(
-                    out=e[:, 0:LAST_SPLIT], in0=e[:, 0:LAST_SPLIT], scalar1=rc[:, 0:1], scalar2=None, op0=ALU.mult
-                )
-                nc.scalar.activation(
-                    out=e[:, LAST_SPLIT:V], in_=e[:, LAST_SPLIT:V], func=ACT.Copy, scale=rc[:, 0:1]
-                )
-                nc.sync.dma_start(out=o0[rows, HEAD_TOKENS : HEAD_TOKENS + LAST_SPLIT], in_=e[:, 0:LAST_SPLIT])
-                nc.sync.dma_start(out=o0[rows, HEAD_TOKENS + LAST_SPLIT : HEAD_TOKENS + V], in_=e[:, LAST_SPLIT:V])
+                cluster = head_last[:, b, 6:7]
+                nc.gpsimd.tensor_copy(out=e[:, 2:8], in_=head_last[:, b, 0:6])
+                nc.gpsimd.tensor_copy(out=e[:, 2056:2062], in_=next_first[:, b, :])
+                if n < 2 * NT - 1:
+                    cuts = (0, 1024, V) if n == 2 * NT - 2 else (0, V)
+                    for lo, hi in zip(cuts[:-1], cuts[1:]):
+                        nc.gpsimd.tensor_scalar(
+                            out=e[:, 8 + lo : 8 + hi], in0=e[:, 8 + lo : 8 + hi],
+                            scalar1=r[:, 0:1], scalar2=cluster, op0=ALU.mult, op1=ALU.mult,
+                        )
+                        store_tail(e, b, lo, hi if hi < V else 2056)
+                else:
+                    rc = stats.tile([P, 1], F32, name="rc")
+                    nc.vector.tensor_scalar(
+                        out=rc[:], in0=r[:], scalar1=cluster, scalar2=None, op0=ALU.mult
+                    )
+                    nc.vector.tensor_scalar(
+                        out=e[:, 8 : 8 + LAST_SPLIT], in0=e[:, 8 : 8 + LAST_SPLIT],
+                        scalar1=rc[:, 0:1], scalar2=None, op0=ALU.mult,
+                    )
+                    nc.scalar.activation(
+                        out=e[:, 8 + LAST_SPLIT : 8 + V], in_=e[:, 8 + LAST_SPLIT : 8 + V], func=ACT.Copy,
+                        scale=rc[:, 0:1],
+                    )
+                    store_tail(e, b, 0, LAST_SPLIT)
+                    store_tail(e, b, LAST_SPLIT, 2056)
 
         first = ["A0", "A1", "B0", "B1", "B2", "B3", "B4", "B5", "B6", "B7"]
         for k in range(5):
@@ -321,27 +341,41 @@ def tile_adaptiveinputsoftmax_pa_kernel(tc, x, head_weight, tail_proj_0, tail_w_
             if n > 0:
                 negate_max(n)
             exps(n)
-            if n > 0:
+            if n > 1:
                 finish(n - 1)
             if n in late_units:
                 regroup(late_units[n], True)
             if n + 1 < 2 * NT:
                 row_max(n + 1, range(1, 4))
+            if n == 0:
+                finish(0)
+            if n in (7, 12):
+                half = slice(0, 4) if n == 7 else slice(4, 8)
+                nc.vector.tensor_copy(
+                    out=next_first[:, half, :].rearrange("p b c -> p (b c)"), in_=banks[("shift", n - 1)][:, 0:24]
+                )
             if n - 1 in late_units:
                 quantise(late_units[n - 1])
             for i in h_tiles.get(n, ()):
                 h_matmuls(i)
             for i in h_tiles.get(n, ()):
                 h_out(i)
-            if n == 9:
+            if n in (6, 11):
+                half = slice(0, 4) if n == 6 else slice(4, 8)
+                shift_bank = new_bank(("shift", n))
+                nc.tensor.matmul(
+                    shift_bank[:, 0:24], lhsT=shift[:], rhs=head_first[:, half, :].rearrange("p b c -> p (b c)"),
+                    start=True, stop=True,
+                )
+            if n == 11:
                 o1_bank = new_bank("o1")
-                nc.tensor.transpose(o1_bank[:, 0:P], cl[:, 1, :], ident[:])
+                nc.tensor.transpose(o1_bank[:, 0:P], head_last[:].rearrange("p b c -> p (b c)"), ident[:])
             if n == 3:
                 h_quantise(0)
             if n == 7:
                 h_quantise(1)
-            if n == 10:
+            if n == 12:
                 o1_sb = keep.tile([P, P], F32)
                 nc.vector.tensor_copy(out=o1_sb[:], in_=banks["o1"][:, 0:P])
-                nc.sync.dma_start(out=o1.rearrange("(i p) o -> i (p o)", p=P), in_=o1_sb[0:NT, :])
+                nc.sync.dma_start(out=o1.rearrange("(i p) o -> i (p o)", p=P), in_=o1_sb[7 : 8 * NT : 8, :])
         finish(2 * NT - 1)

@@ -244,6 +244,9 @@ def tile_adaptiveinputsoftmax_pa_kernel(tc, x, head_weight, tail_proj_0, tail_w_
             nc.scalar.activation(
                 out=e[:, 8 : 8 + V], in_=e[:, 8 : 8 + V], func=ACT.Exp, bias=small[("negm", n)][:, 0:1], scale=1.0, accum_out=s[:]
             )
+            if n >= NT:
+                nc.scalar.copy(out=e[:, 2:8], in_=head_last[:, n % NT, 0:6])
+                nc.scalar.copy(out=e[:, 2056:2062], in_=next_first[:, n % NT, :])
 
         def store_head(e, b, lo, hi):
             for i in range(4):
@@ -282,12 +285,11 @@ def tile_adaptiveinputsoftmax_pa_kernel(tc, x, head_weight, tail_proj_0, tail_w_
                 )
             else:
                 cluster = head_last[:, b, 6:7]
-                nc.gpsimd.tensor_copy(out=e[:, 2:8], in_=head_last[:, b, 0:6])
-                nc.gpsimd.tensor_copy(out=e[:, 2056:2062], in_=next_first[:, b, :])
                 if n < 2 * NT - 1:
-                    cuts = (0, 1024, V) if n == 2 * NT - 2 else (0, V)
+                    engine = nc.vector if n == 2 * NT - 2 else nc.gpsimd
+                    cuts = (0, V)
                     for lo, hi in zip(cuts[:-1], cuts[1:]):
-                        nc.gpsimd.tensor_scalar(
+                        engine.tensor_scalar(
                             out=e[:, 8 + lo : 8 + hi], in0=e[:, 8 + lo : 8 + hi],
                             scalar1=r[:, 0:1], scalar2=cluster, op0=ALU.mult, op1=ALU.mult,
                         )
@@ -305,8 +307,7 @@ def tile_adaptiveinputsoftmax_pa_kernel(tc, x, head_weight, tail_proj_0, tail_w_
                         out=e[:, 8 + LAST_SPLIT : 8 + V], in_=e[:, 8 + LAST_SPLIT : 8 + V], func=ACT.Copy,
                         scale=rc[:, 0:1],
                     )
-                    store_tail(e, b, 0, LAST_SPLIT)
-                    store_tail(e, b, LAST_SPLIT, 2056)
+                    store_tail(e, b, 0, 2056)
 
         first = ["A0", "A1", "B0", "B1", "B2", "B3", "B4", "B5", "B6", "B7"]
         for k in range(5):
@@ -326,41 +327,45 @@ def tile_adaptiveinputsoftmax_pa_kernel(tc, x, head_weight, tail_proj_0, tail_w_
         logits(1)
         regroup("C1", True)
         row_max(0)
-        regroup("C0", False)
         negate_max(0)
+        regroup("C0", False)
+        exps(0)
+        regroup("C2", True)
+        row_max(1, (0, 1))
         quantise("C1")
         quantise("C0")
+        finish(0)
+        row_max(1, (2, 3))
 
         h_tiles = {1: (0, 1), 2: (2, 3), 5: (4, 5), 6: (6, 7)}
-        late_units = {0: "C2", 3: "C3"}
+        late_units = {3: "C3"}
+        late_quantises = {1: "C2", 4: "C3"}
         for n in range(2 * NT):
             if n + 2 < 2 * NT:
                 logits(n + 2)
-            if n + 1 < 2 * NT:
+            if 1 < n + 1 < 2 * NT:
                 row_max(n + 1, range(1))
             if n > 0:
                 negate_max(n)
-            exps(n)
+                exps(n)
             if n > 1:
                 finish(n - 1)
             if n in late_units:
                 regroup(late_units[n], True)
-            if n + 1 < 2 * NT:
+            if 1 < n + 1 < 2 * NT:
                 row_max(n + 1, range(1, 4))
-            if n == 0:
-                finish(0)
-            if n in (7, 12):
+            if n in (7, 11):
                 half = slice(0, 4) if n == 7 else slice(4, 8)
                 nc.vector.tensor_copy(
                     out=next_first[:, half, :].rearrange("p b c -> p (b c)"), in_=banks[("shift", n - 1)][:, 0:24]
                 )
-            if n - 1 in late_units:
-                quantise(late_units[n - 1])
+            if n in late_quantises:
+                quantise(late_quantises[n])
             for i in h_tiles.get(n, ()):
                 h_matmuls(i)
             for i in h_tiles.get(n, ()):
                 h_out(i)
-            if n in (6, 11):
+            if n in (6, 10):
                 half = slice(0, 4) if n == 6 else slice(4, 8)
                 shift_bank = new_bank(("shift", n))
                 nc.tensor.matmul(

@@ -19,6 +19,7 @@ V = 2048
 P0 = 512
 NT = TOKENS // P
 HEAD_TOKENS = 2046
+WIDTH = HEAD_TOKENS + V
 BANK = 512
 LAST_SPLIT = 1344
 BIG_BUFS = 13
@@ -31,7 +32,8 @@ def tile_adaptiveinputsoftmax_pa_kernel(tc, x, head_weight, tail_proj_0, tail_w_
     xf = x.flatten_outer_dims()
     o0 = out_0.flatten_outer_dims()
     o1 = out_1.flatten_outer_dims()
-    o0_rows4 = o0.rearrange("(b q i) c -> b q (i c)", q=P // 4, i=4)
+    x_view = xf.rearrange("(p i) k -> p i k", i=NT)
+    probs = o0.rearrange("(p i) c -> p (i c)", i=NT)
 
     with ExitStack() as ctx:
         ctx.enter_context(tc.manual_schedule())
@@ -63,11 +65,8 @@ def tile_adaptiveinputsoftmax_pa_kernel(tc, x, head_weight, tail_proj_0, tail_w_
             x_part = big.tile([P, 4, D], BF16, tag="big", name="x_part")
             x_raw[b] = x_part
             for a in range(2):
-                t0 = 512 * b + 256 * a
-                nc.sync.dma_start(
-                    out=x_part[:, 2 * a : 2 * a + 2, :],
-                    in_=xf[t0 : t0 + 256, :].rearrange("(i p) k -> p i k", p=P),
-                )
+                i0 = 4 * b + 2 * a
+                nc.sync.dma_start(out=x_part[:, 2 * a : 2 * a + 2, :], in_=x_view[:, i0 : i0 + 2, :])
         tw_raw = {}
         for hf in range(2):
             tw_part = big.tile([P, 4, 1024], BF16, tag="big", name="tw_part")
@@ -81,15 +80,10 @@ def tile_adaptiveinputsoftmax_pa_kernel(tc, x, head_weight, tail_proj_0, tail_w_
         warm_out = keep.tile([P, 1], F32)
         nc.vector.memset(warm_in[:], 0.0)
         nc.scalar.activation(out=warm_out[:], in_=warm_in[:], func=ACT.Exp)
-        head_first = keep.tile([P, NT, 6], F32)
-        head_last = keep.tile([P, 2 * NT, 8], F32)
-        nc.vector.memset(head_last[:], 0.0)
-        next_first = keep.tile([P, NT, 6], F32)
+        head_first = keep.tile([P, NT, 8], F32)
+        head_last = keep.tile([P, NT, 8], F32)
         ident = keep.tile([P, P], F32)
         make_identity(nc, ident[:])
-        shift = keep.tile([P, P], F32)
-        nc.vector.memset(shift[:], 0.0)
-        nc.vector.tensor_copy(out=shift[:, 0 : P - 1], in_=ident[:, 1:P])
 
         x_codes = keep.tile([P, NT, 2 * P], U32, align_bytes=64)
         x_scales = keep.tile([P, NT, 2 * P], U8, align_bytes=64)
@@ -244,56 +238,50 @@ def tile_adaptiveinputsoftmax_pa_kernel(tc, x, head_weight, tail_proj_0, tail_w_
             nc.scalar.activation(
                 out=e[:, 8 : 8 + V], in_=e[:, 8 : 8 + V], func=ACT.Exp, bias=small[("negm", n)][:, 0:1], scale=1.0, accum_out=s[:]
             )
-            if n >= NT:
-                nc.scalar.copy(out=e[:, 2:8], in_=head_last[:, n % NT, 0:6])
-                nc.scalar.copy(out=e[:, 2056:2062], in_=next_first[:, n % NT, :])
+            if n >= NT and n % 4 < 3:
+                i = n % NT
+                nc.scalar.copy(out=e[:, 2:8], in_=head_last[:, i, 0:6])
+                nc.scalar.copy(out=e[:, 2056:2062], in_=head_first[:, i + 1, 0:6])
 
-        def store_head(e, b, lo, hi):
-            for i in range(4):
-                nc.sync.dma_start(
-                    out=o0_rows4[b, :, 4096 * i + lo : 4096 * i + hi],
-                    in_=e[i:P:4, 8 + 2 * i + lo : 8 + 2 * i + hi],
-                )
+        def store_head(e, i, lo, hi):
+            skip = 2 * (i % 4)
+            c0 = WIDTH * i + skip
+            nc.sync.dma_start(out=probs[:, c0 + lo : c0 + hi], in_=e[:, 8 + skip + lo : 8 + skip + hi])
 
-        def store_tail(e, b, lo, hi):
-            for i in range(4):
-                end = min(hi, 2056 if i < 3 else 2048)
-                nc.sync.dma_start(
-                    out=o0_rows4[b, :, 4096 * i + 2040 + lo : 4096 * i + 2040 + end],
-                    in_=e[i:P:4, 2 + 2 * i + lo : 2 + 2 * i + end],
-                )
+        def store_tail(e, i):
+            skip = 2 * (i % 4)
+            c0 = WIDTH * i + 2040 + skip
+            length = 2056 if skip < 6 else 2048
+            nc.sync.dma_start(out=probs[:, c0 : c0 + length], in_=e[:, 2 + skip : 2 + skip + length])
 
         def finish(n):
-            b = n % NT
+            i = n % NT
             e = small[("e", n)]
             s = small[("s", n)]
             r = stats.tile([P, 1], F32, name="r")
             nc.vector.reciprocal(out=r[:], in_=s[:])
             if n < NT:
+                nc.gpsimd.tensor_scalar(
+                    out=head_last[:, i, :], in0=e[:, V : V + 8], scalar1=r[:, 0:1], scalar2=0.0,
+                    op0=ALU.mult, op1=ALU.add,
+                )
                 steps = ((0, 1032, 0, 1024), (1032, 2046, 1024, 2040)) if n == 0 else ((0, 2046, 0, 2040),)
                 for c0, c1, lo, hi in steps:
                     nc.gpsimd.tensor_scalar(
                         out=e[:, 8 + c0 : 8 + c1], in0=e[:, 8 + c0 : 8 + c1],
                         scalar1=r[:, 0:1], scalar2=0.0, op0=ALU.mult, op1=ALU.add,
                     )
-                    store_head(e, b, lo, hi)
-                nc.gpsimd.tensor_copy(out=head_first[:, b, :], in_=e[:, 8:14])
-                nc.gpsimd.tensor_copy(out=head_last[:, b, 0:6], in_=e[:, 2048:2054])
-                nc.gpsimd.tensor_scalar(
-                    out=head_last[:, b, 6:8], in0=e[:, 2054:2056], scalar1=r[:, 0:1], scalar2=0.0,
-                    op0=ALU.mult, op1=ALU.add,
-                )
+                    store_head(e, i, lo, hi)
+                if i % 4 > 0:
+                    nc.gpsimd.tensor_copy(out=head_first[:, i, 0:6], in_=e[:, 8:14])
             else:
-                cluster = head_last[:, b, 6:7]
+                cluster = head_last[:, i, 6:7]
                 if n < 2 * NT - 1:
                     engine = nc.vector if n == 2 * NT - 2 else nc.gpsimd
-                    cuts = (0, V)
-                    for lo, hi in zip(cuts[:-1], cuts[1:]):
-                        engine.tensor_scalar(
-                            out=e[:, 8 + lo : 8 + hi], in0=e[:, 8 + lo : 8 + hi],
-                            scalar1=r[:, 0:1], scalar2=cluster, op0=ALU.mult, op1=ALU.mult,
-                        )
-                        store_tail(e, b, lo, hi if hi < V else 2056)
+                    engine.tensor_scalar(
+                        out=e[:, 8 : 8 + V], in0=e[:, 8 : 8 + V],
+                        scalar1=r[:, 0:1], scalar2=cluster, op0=ALU.mult, op1=ALU.mult,
+                    )
                 else:
                     rc = stats.tile([P, 1], F32, name="rc")
                     nc.vector.tensor_scalar(
@@ -307,7 +295,7 @@ def tile_adaptiveinputsoftmax_pa_kernel(tc, x, head_weight, tail_proj_0, tail_w_
                         out=e[:, 8 + LAST_SPLIT : 8 + V], in_=e[:, 8 + LAST_SPLIT : 8 + V], func=ACT.Copy,
                         scale=rc[:, 0:1],
                     )
-                    store_tail(e, b, 0, 2056)
+                store_tail(e, i)
 
         first = ["A0", "A1", "B0", "B1", "B2", "B3", "B4", "B5", "B6", "B7"]
         for k in range(5):
@@ -354,33 +342,18 @@ def tile_adaptiveinputsoftmax_pa_kernel(tc, x, head_weight, tail_proj_0, tail_w_
                 regroup(late_units[n], True)
             if 1 < n + 1 < 2 * NT:
                 row_max(n + 1, range(1, 4))
-            if n in (7, 11):
-                half = slice(0, 4) if n == 7 else slice(4, 8)
-                nc.vector.tensor_copy(
-                    out=next_first[:, half, :].rearrange("p b c -> p (b c)"), in_=banks[("shift", n - 1)][:, 0:24]
-                )
             if n in late_quantises:
                 quantise(late_quantises[n])
             for i in h_tiles.get(n, ()):
                 h_matmuls(i)
             for i in h_tiles.get(n, ()):
                 h_out(i)
-            if n in (6, 10):
-                half = slice(0, 4) if n == 6 else slice(4, 8)
-                shift_bank = new_bank(("shift", n))
-                nc.tensor.matmul(
-                    shift_bank[:, 0:24], lhsT=shift[:], rhs=head_first[:, half, :].rearrange("p b c -> p (b c)"),
-                    start=True, stop=True,
-                )
-            if n == 11:
-                o1_bank = new_bank("o1")
-                nc.tensor.transpose(o1_bank[:, 0:P], head_last[:].rearrange("p b c -> p (b c)"), ident[:])
             if n == 3:
                 h_quantise(0)
             if n == 7:
                 h_quantise(1)
-            if n == 12:
-                o1_sb = keep.tile([P, P], F32)
-                nc.vector.tensor_copy(out=o1_sb[:], in_=banks["o1"][:, 0:P])
-                nc.sync.dma_start(out=o1.rearrange("(i p) o -> i (p o)", p=P), in_=o1_sb[7 : 8 * NT : 8, :])
+            if n == 10:
+                other = keep.tile([P, NT], F32)
+                nc.scalar.copy(out=other[:], in_=head_last[:, :, 7])
+                nc.sync.dma_start(out=o1.rearrange("(p i) o -> p (i o)", i=NT), in_=other[:])
         finish(2 * NT - 1)

@@ -23,6 +23,7 @@ WIDTH = HEAD_TOKENS + V
 BANK = 512
 LAST_SPLIT = 1344
 BIG_BUFS = 13
+BY_SCALAR = ('A1', 'B1', 'B2', 'B5', 'B6', 'C1', 'C2', 'C3')
 
 FLOPS = 2 * TOKENS * (D * V + D * P0 + P0 * V)
 
@@ -44,31 +45,34 @@ def tile_adaptiveinputsoftmax_pa_kernel(tc, x, head_weight, tail_proj_0, tail_w_
         psum = ctx.enter_context(tc.psum_pool(name="psum", bufs=8))
 
         tp_raw = big.tile([P, 2, 4, P0], BF16, tag="big", name="tp_raw")
-        for g in range(2):
+        x_raw = {}
+        hw_raw = {}
+        tw_raw = {}
+
+        def load_tp(g):
             nc.sync.dma_start(
                 out=tp_raw[:, g, :, :],
                 in_=tail_proj_0[512 * g : 512 * g + 512, :].rearrange("(p j) c -> p j c", j=4),
             )
-        hw_raw = {}
-        for g in range(2):
-            for hf in range(2):
-                hw_part = big.tile([P, 4, 1024], BF16, tag="big", name="hw_part")
-                hw_raw[(g, hf)] = hw_part
-                nc.sync.dma_start(
-                    out=hw_part[:],
-                    in_=head_weight[512 * g : 512 * g + 512, 1024 * hf : 1024 * hf + 1024].rearrange(
-                        "(p j) c -> p j c", j=4
-                    ),
-                )
-        x_raw = {}
-        for b in range(2):
-            x_part = big.tile([P, 4, D], BF16, tag="big", name="x_part")
-            x_raw[b] = x_part
-            for a in range(2):
-                i0 = 4 * b + 2 * a
-                nc.sync.dma_start(out=x_part[:, 2 * a : 2 * a + 2, :], in_=x_view[:, i0 : i0 + 2, :])
-        tw_raw = {}
-        for hf in range(2):
+
+        def load_x(b, a):
+            if a == 0:
+                x_part = big.tile([P, 4, D], BF16, tag="big", name="x_part")
+                x_raw[b] = x_part
+            i0 = 4 * b + 2 * a
+            nc.sync.dma_start(out=x_raw[b][:, 2 * a : 2 * a + 2, :], in_=x_view[:, i0 : i0 + 2, :])
+
+        def load_hw(g, hf):
+            hw_part = big.tile([P, 4, 1024], BF16, tag="big", name="hw_part")
+            hw_raw[(g, hf)] = hw_part
+            nc.sync.dma_start(
+                out=hw_part[:],
+                in_=head_weight[512 * g : 512 * g + 512, 1024 * hf : 1024 * hf + 1024].rearrange(
+                    "(p j) c -> p j c", j=4
+                ),
+            )
+
+        def load_tw(hf):
             tw_part = big.tile([P, 4, 1024], BF16, tag="big", name="tw_part")
             tw_raw[hf] = tw_part
             nc.sync.dma_start(
@@ -76,6 +80,18 @@ def tile_adaptiveinputsoftmax_pa_kernel(tc, x, head_weight, tail_proj_0, tail_w_
                 in_=tail_w_0[:, 1024 * hf : 1024 * hf + 1024].rearrange("(p j) n -> p j n", j=4),
             )
 
+        load_tp(0)
+        load_tp(1)
+        load_x(0, 0)
+        load_hw(0, 0)
+        load_hw(0, 1)
+        load_hw(1, 0)
+        load_hw(1, 1)
+        load_x(0, 1)
+        load_x(1, 0)
+        load_x(1, 1)
+        load_tw(0)
+        load_tw(1)
         warm_in = keep.tile([P, 1], F32)
         warm_out = keep.tile([P, 1], F32)
         nc.vector.memset(warm_in[:], 0.0)
@@ -112,7 +128,7 @@ def tile_adaptiveinputsoftmax_pa_kernel(tc, x, head_weight, tail_proj_0, tail_w_
             units["C%d" % c] = (tw_raw[c // 2][:, :, part], tw_codes[:, cols], tw_scales[:, cols])
         grouped = {}
 
-        def regroup(u, on_scalar):
+        def regroup(u):
             gw = gwp.tile([P, BANK, 4], BF16, align_bytes=64, name="gw")
             grouped[u] = gw
             if u[0] == "A":
@@ -121,7 +137,7 @@ def tile_adaptiveinputsoftmax_pa_kernel(tc, x, head_weight, tail_proj_0, tail_w_
             else:
                 dst_v = gw[:].rearrange("p (c i) t -> p c t i", i=4)
                 src_v = units[u][0].rearrange("p t (c i) -> p c t i", i=4)
-            if on_scalar:
+            if u in BY_SCALAR:
                 nc.scalar.copy(out=dst_v, in_=src_v)
             else:
                 nc.vector.tensor_copy(out=dst_v, in_=src_v)
@@ -248,11 +264,11 @@ def tile_adaptiveinputsoftmax_pa_kernel(tc, x, head_weight, tail_proj_0, tail_w_
             c0 = WIDTH * i + skip
             nc.sync.dma_start(out=probs[:, c0 + lo : c0 + hi], in_=e[:, 8 + skip + lo : 8 + skip + hi])
 
-        def store_tail(e, i):
+        def store_tail(e, i, lo=0, hi=2056):
             skip = 2 * (i % 4)
             c0 = WIDTH * i + 2040 + skip
-            length = 2056 if skip < 6 else 2048
-            nc.sync.dma_start(out=probs[:, c0 : c0 + length], in_=e[:, 2 + skip : 2 + skip + length])
+            end = min(hi, 2056 if skip < 6 else 2048)
+            nc.sync.dma_start(out=probs[:, c0 + lo : c0 + end], in_=e[:, 2 + skip + lo : 2 + skip + end])
 
         def finish(n):
             i = n % NT
@@ -265,7 +281,7 @@ def tile_adaptiveinputsoftmax_pa_kernel(tc, x, head_weight, tail_proj_0, tail_w_
                     out=head_last[:, i, :], in0=e[:, V : V + 8], scalar1=r[:, 0:1], scalar2=0.0,
                     op0=ALU.mult, op1=ALU.add,
                 )
-                steps = ((0, 1032, 0, 1024), (1032, 2046, 1024, 2040)) if n == 0 else ((0, 2046, 0, 2040),)
+                steps = ((0, 1032, 0, 1024), (1032, 2046, 1024, 2040))
                 for c0, c1, lo, hi in steps:
                     nc.gpsimd.tensor_scalar(
                         out=e[:, 8 + c0 : 8 + c1], in0=e[:, 8 + c0 : 8 + c1],
@@ -278,10 +294,13 @@ def tile_adaptiveinputsoftmax_pa_kernel(tc, x, head_weight, tail_proj_0, tail_w_
                 cluster = head_last[:, i, 6:7]
                 if n < 2 * NT - 1:
                     engine = nc.vector if n == 2 * NT - 2 else nc.gpsimd
-                    engine.tensor_scalar(
-                        out=e[:, 8 : 8 + V], in0=e[:, 8 : 8 + V],
-                        scalar1=r[:, 0:1], scalar2=cluster, op0=ALU.mult, op1=ALU.mult,
-                    )
+                    cuts = (0, 1024, V) if n < 2 * NT - 2 else (0, V)
+                    for lo, hi in zip(cuts[:-1], cuts[1:]):
+                        engine.tensor_scalar(
+                            out=e[:, 8 + lo : 8 + hi], in0=e[:, 8 + lo : 8 + hi],
+                            scalar1=r[:, 0:1], scalar2=cluster, op0=ALU.mult, op1=ALU.mult,
+                        )
+                        store_tail(e, i, lo, hi if hi < V else 2056)
                 else:
                     rc = stats.tile([P, 1], F32, name="rc")
                     nc.vector.tensor_scalar(
@@ -295,63 +314,71 @@ def tile_adaptiveinputsoftmax_pa_kernel(tc, x, head_weight, tail_proj_0, tail_w_
                         out=e[:, 8 + LAST_SPLIT : 8 + V], in_=e[:, 8 + LAST_SPLIT : 8 + V], func=ACT.Copy,
                         scale=rc[:, 0:1],
                     )
-                store_tail(e, i)
+                    store_tail(e, i, 0, LAST_SPLIT)
+                    store_tail(e, i, LAST_SPLIT)
 
-        first = ["A0", "A1", "B0", "B1", "B2", "B3", "B4", "B5", "B6", "B7"]
-        for k in range(5):
-            regroup(first[2 * k + 1], True)
-            regroup(first[2 * k], False)
-            if k > 0:
-                quantise(first[2 * k - 1])
-            quantise(first[2 * k])
-        for i in range(NT):
-            x_transpose(i)
-        for i in range(NT):
-            x_out(i)
-        quantise("B7")
-        for i in range(NT):
-            x_quantise(i)
+        first = ("A0", "A1", "B0", "B1", "B2", "B3", "B4", "B5", "B6", "B7")
+        for k, u in enumerate(first):
+            regroup(u)
+            if k >= 1:
+                quantise(first[k - 1])
+            if k == 2:
+                for i in range(2):
+                    x_transpose(i)
+                    x_out(i)
+            if k == 3:
+                for i in range(2):
+                    x_quantise(i)
+            if k == 9:
+                for i in range(2, 4):
+                    x_transpose(i)
+                    x_out(i)
+        for u in first[-1:]:
+            quantise(u)
         logits(0)
-        logits(1)
-        regroup("C1", True)
+        for i in range(4, NT):
+            x_transpose(i)
+            x_out(i)
         row_max(0)
         negate_max(0)
-        regroup("C0", False)
-        exps(0)
-        regroup("C2", True)
-        row_max(1, (0, 1))
-        quantise("C1")
-        quantise("C0")
-        finish(0)
-        row_max(1, (2, 3))
+        for i in range(2, 4):
+            x_quantise(i)
+        for u in ('C0',):
+            regroup(u)
 
-        h_tiles = {1: (0, 1), 2: (2, 3), 5: (4, 5), 6: (6, 7)}
-        late_units = {3: "C3"}
-        late_quantises = {1: "C2", 4: "C3"}
+        h_tiles = {2: (0, 1), 4: (2, 3), 5: (4, 5), 6: (6, 7)}
+        late_units = {0: ('C1',), 1: ('C2',), 3: ('C3',)}
+        late_quantises = {0: ('C0',), 1: ('C1',), 2: ('C2',), 4: ('C3',)}
         for n in range(2 * NT):
-            if n + 2 < 2 * NT:
-                logits(n + 2)
-            if 1 < n + 1 < 2 * NT:
-                row_max(n + 1, range(1))
-            if n > 0:
-                negate_max(n)
-                exps(n)
-            if n > 1:
-                finish(n - 1)
-            if n in late_units:
-                regroup(late_units[n], True)
-            if 1 < n + 1 < 2 * NT:
-                row_max(n + 1, range(1, 4))
-            if n in late_quantises:
-                quantise(late_quantises[n])
+            exps(n)
+            if n + 1 < 2 * NT:
+                logits(n + 1)
+            for u in late_units.get(n, ()):
+                if u in BY_SCALAR:
+                    regroup(u)
             for i in h_tiles.get(n, ()):
                 h_matmuls(i)
             for i in h_tiles.get(n, ()):
                 h_out(i)
-            if n == 3:
+            if n + 1 < 2 * NT:
+                row_max(n + 1, range(2))
+            if n > 0:
+                finish(n - 1)
+            if n + 1 < 2 * NT:
+                row_max(n + 1, range(2, 4))
+                negate_max(n + 1)
+            if n == 0:
+                for i in range(4, NT):
+                    x_quantise(i)
+            for u in late_quantises.get(n, ()):
+                quantise(u)
+            if n == 5:
                 h_quantise(0)
             if n == 7:
                 h_quantise(1)
+            for u in late_units.get(n, ()):
+                if u not in BY_SCALAR:
+                    regroup(u)
             if n == 10:
                 other = keep.tile([P, NT], F32)
                 nc.scalar.copy(out=other[:], in_=head_last[:, :, 7])

from contextlib import ExitStack

import concourse.mybir as mybir
from concourse.masks import make_identity

F32 = mybir.dt.float32
BF16 = mybir.dt.bfloat16
U32 = mybir.dt.uint32
U8 = mybir.dt.uint8
FP8X4 = mybir.dt.float8_e4m3fn_x4
ALU = mybir.AluOpType
ACT = mybir.ActivationFunctionType
AX = mybir.AxisListType

P = 128
TOKENS = 1024
D = 1024
V = 2048
P0 = 512
NT = TOKENS // P
HEAD_TOKENS = 2046
WIDTH = HEAD_TOKENS + V
BANK = 512
LAST_SPLIT = 1344
BIG_BUFS = 13
BY_SCALAR = ('A1', 'B1', 'B2', 'B5', 'B6', 'C1', 'C2', 'C3')

FLOPS = 2 * TOKENS * (D * V + D * P0 + P0 * V)


def tile_adaptiveinputsoftmax_pa_kernel(tc, x, head_weight, tail_proj_0, tail_w_0, out_0, out_1):
    nc = tc.nc
    xf = x.flatten_outer_dims()
    o0 = out_0.flatten_outer_dims()
    o1 = out_1.flatten_outer_dims()
    x_view = xf.rearrange("(p i) k -> p i k", i=NT)
    probs = o0.rearrange("(p i) c -> p (i c)", i=NT)

    with ExitStack() as ctx:
        ctx.enter_context(tc.manual_schedule())
        keep = ctx.enter_context(tc.tile_pool(name="keep", bufs=1))
        gwp = ctx.enter_context(tc.tile_pool(name="gwp", bufs=5))
        big = ctx.enter_context(tc.tile_pool(name="big", bufs=BIG_BUFS))
        stats = ctx.enter_context(tc.tile_pool(name="stats", bufs=6))
        psum = ctx.enter_context(tc.psum_pool(name="psum", bufs=8))

        tp_raw = big.tile([P, 2, 4, P0], BF16, tag="big", name="tp_raw")
        x_raw = {}
        hw_raw = {}
        tw_raw = {}

        def load_tp(g):
            nc.sync.dma_start(
                out=tp_raw[:, g, :, :],
                in_=tail_proj_0[512 * g : 512 * g + 512, :].rearrange("(p j) c -> p j c", j=4),
            )

        def load_x(b, a):
            if a == 0:
                x_part = big.tile([P, 4, D], BF16, tag="big", name="x_part")
                x_raw[b] = x_part
            i0 = 4 * b + 2 * a
            nc.sync.dma_start(out=x_raw[b][:, 2 * a : 2 * a + 2, :], in_=x_view[:, i0 : i0 + 2, :])

        def load_hw(g, hf):
            hw_part = big.tile([P, 4, 1024], BF16, tag="big", name="hw_part")
            hw_raw[(g, hf)] = hw_part
            nc.sync.dma_start(
                out=hw_part[:],
                in_=head_weight[512 * g : 512 * g + 512, 1024 * hf : 1024 * hf + 1024].rearrange(
                    "(p j) c -> p j c", j=4
                ),
            )

        def load_tw(hf):
            tw_part = big.tile([P, 4, 1024], BF16, tag="big", name="tw_part")
            tw_raw[hf] = tw_part
            nc.sync.dma_start(
                out=tw_part[:],
                in_=tail_w_0[:, 1024 * hf : 1024 * hf + 1024].rearrange("(p j) n -> p j n", j=4),
            )

        load_tp(0)
        load_tp(1)
        load_x(0, 0)
        load_hw(0, 0)
        load_hw(0, 1)
        load_hw(1, 0)
        load_hw(1, 1)
        load_x(0, 1)
        load_x(1, 0)
        load_x(1, 1)
        load_tw(0)
        load_tw(1)
        warm_in = keep.tile([P, 1], F32)
        warm_out = keep.tile([P, 1], F32)
        nc.vector.memset(warm_in[:], 0.0)
        nc.scalar.activation(out=warm_out[:], in_=warm_in[:], func=ACT.Exp)
        head_first = keep.tile([P, NT, 8], F32)
        head_last = keep.tile([P, NT, 8], F32)
        ident = keep.tile([P, P], F32)
        make_identity(nc, ident[:])

        x_codes = keep.tile([P, NT, 2 * P], U32, align_bytes=64)
        x_scales = keep.tile([P, NT, 2 * P], U8, align_bytes=64)
        tp_codes = keep.tile([P, 2, P0], U32, align_bytes=64)
        tp_scales = keep.tile([P, 2, P0], U8, align_bytes=64)
        hw_codes = keep.tile([P, 2, V], U32, align_bytes=64)
        hw_scales = keep.tile([P, 2, V], U8, align_bytes=64)
        tw_codes = keep.tile([P, V], U32, align_bytes=64)
        tw_scales = keep.tile([P, V], U8, align_bytes=64)
        gx = keep.tile([P, NT, 2, P, 2], F32, align_bytes=64)
        gh = keep.tile([P, NT, P, 4], BF16, align_bytes=64)
        h_codes = keep.tile([P, NT * P], U32, align_bytes=64)
        h_scales = keep.tile([P, NT * P], U8, align_bytes=64)

        units = {}
        for g in range(2):
            units["A%d" % g] = (tp_raw[:, g, :, :], tp_codes[:, g, :], tp_scales[:, g, :])
        for n in range(8):
            g, c = divmod(n, 4)
            cols = slice(BANK * c, BANK * c + BANK)
            part = slice(BANK * (c % 2), BANK * (c % 2) + BANK)
            units["B%d" % n] = (hw_raw[(g, c // 2)][:, :, part], hw_codes[:, g, cols], hw_scales[:, g, cols])
        for c in range(4):
            cols = slice(BANK * c, BANK * c + BANK)
            part = slice(BANK * (c % 2), BANK * (c % 2) + BANK)
            units["C%d" % c] = (tw_raw[c // 2][:, :, part], tw_codes[:, cols], tw_scales[:, cols])
        grouped = {}

        def regroup(u):
            gw = gwp.tile([P, BANK, 4], BF16, align_bytes=64, name="gw")
            grouped[u] = gw
            if u[0] == "A":
                dst_v = gw[:].rearrange("p (t m) j -> p t m j", t=4)
                src_v = units[u][0].rearrange("p j (m t) -> p t m j", t=4)
            else:
                dst_v = gw[:].rearrange("p (c i) t -> p c t i", i=4)
                src_v = units[u][0].rearrange("p t (c i) -> p c t i", i=4)
            if u in BY_SCALAR:
                nc.scalar.copy(out=dst_v, in_=src_v)
            else:
                nc.vector.tensor_copy(out=dst_v, in_=src_v)

        def quantise(u):
            nc.vector.quantize_mx(
                out=units[u][1].bitcast(FP8X4),
                scales=units[u][2],
                in_=grouped[u][:].rearrange("p w t -> p (w t)"),
            )

        banks = {}

        def new_bank(key):
            bank = psum.tile([P, BANK], F32, tag="bank", name="bank")
            banks[key] = bank
            return bank

        def x_transpose(i):
            xw = x_raw[i // 4][:, i % 4, :].bitcast(F32)
            bank = new_bank(("x", i))
            for c in range(4):
                g, u = divmod(c, 2)
                nc.tensor.transpose(
                    bank[:, P * c : P * c + P], xw[:, 256 * g + u : 256 * (g + 1) : 2], ident[:]
                )

        def x_out(i):
            nc.scalar.copy(
                out=gx[:, i, :, :, :], in_=banks[("x", i)][:].rearrange("p (g u r) -> p g r u", g=2, u=2)
            )

        def x_quantise(i):
            nc.vector.quantize_mx(
                out=x_codes[:, i, :].bitcast(FP8X4),
                scales=x_scales[:, i, :],
                in_=gx[:, i, :, :, :].rearrange("p g r u -> p (g r u)").bitcast(BF16),
            )

        def h_matmuls(i):
            bank = new_bank(("h", i))
            for j in range(4):
                for g in range(2):
                    nc.tensor.matmul_mx(
                        out=bank[:, P * j : P * j + P],
                        lhsT=tp_codes[:, g, P * j : P * j + P].bitcast(FP8X4),
                        lhsT_scale=tp_scales[:, g, P * j : P * j + P],
                        rhs=x_codes[:, i, P * g : P * g + P].bitcast(FP8X4),
                        rhs_scale=x_scales[:, i, P * g : P * g + P],
                        start=(g == 0),
                        stop=(g == 1),
                    )

        def h_out(i):
            nc.scalar.copy(out=gh[:, i, :, :], in_=banks[("h", i)][:].rearrange("p (j r) -> p r j", j=4))

        def h_quantise(a):
            nc.vector.quantize_mx(
                out=h_codes[:, 512 * a : 512 * a + 512].bitcast(FP8X4),
                scales=h_scales[:, 512 * a : 512 * a + 512],
                in_=gh[:, 4 * a : 4 * a + 4, :, :].rearrange("p i r j -> p (i r j)"),
            )

        def logits(n):
            i = n % NT
            for c in range(4):
                cols = slice(BANK * c, BANK * c + BANK)
                bank = new_bank((n, c))
                if n < NT:
                    for g in range(2):
                        nc.tensor.matmul_mx(
                            out=bank[:],
                            lhsT=x_codes[:, i, P * g : P * g + P].bitcast(FP8X4),
                            lhsT_scale=x_scales[:, i, P * g : P * g + P],
                            rhs=hw_codes[:, g, cols].bitcast(FP8X4),
                            rhs_scale=hw_scales[:, g, cols],
                            start=(g == 0),
                            stop=(g == 1),
                        )
                else:
                    nc.tensor.matmul_mx(
                        out=bank[:],
                        lhsT=h_codes[:, P * i : P * i + P].bitcast(FP8X4),
                        lhsT_scale=h_scales[:, P * i : P * i + P],
                        rhs=tw_codes[:, cols].bitcast(FP8X4),
                        rhs_scale=tw_scales[:, cols],
                        start=True,
                        stop=True,
                    )

        small = {}

        def row_max(n, chunks=range(4)):
            if chunks[0] == 0:
                small[("e", n)] = big.tile([P, V + 16], F32, tag="big", name="e")
                small[("m4", n)] = stats.tile([P, 4], F32, name="m4")
            e = small[("e", n)]
            m4 = small[("m4", n)]
            for c in chunks:
                nc.vector.tensor_scalar(
                    out=e[:, 8 + BANK * c : 8 + BANK * c + BANK], in0=banks[(n, c)][:], scalar1=1.0, scalar2=None,
                    op0=ALU.mult, op1=ALU.max, accum_out=m4[:, c : c + 1],
                )

        def negate_max(n):
            negm = stats.tile([P, 1], F32, name="negm")
            nc.vector.tensor_reduce(out=negm[:], in_=small[("m4", n)][:], axis=AX.X, op=ALU.max, negate=True)
            small[("negm", n)] = negm

        def exps(n):
            e = small[("e", n)]
            s = stats.tile([P, 1], F32, name="s")
            small[("s", n)] = s
            nc.scalar.activation(
                out=e[:, 8 : 8 + V], in_=e[:, 8 : 8 + V], func=ACT.Exp, bias=small[("negm", n)][:, 0:1], scale=1.0, accum_out=s[:]
            )
            if n >= NT and n % 4 < 3:
                i = n % NT
                nc.scalar.copy(out=e[:, 2:8], in_=head_last[:, i, 0:6])
                nc.scalar.copy(out=e[:, 2056:2062], in_=head_first[:, i + 1, 0:6])

        def store_head(e, i, lo, hi):
            skip = 2 * (i % 4)
            c0 = WIDTH * i + skip
            nc.sync.dma_start(out=probs[:, c0 + lo : c0 + hi], in_=e[:, 8 + skip + lo : 8 + skip + hi])

        def store_tail(e, i, lo=0, hi=2056):
            skip = 2 * (i % 4)
            c0 = WIDTH * i + 2040 + skip
            end = min(hi, 2056 if skip < 6 else 2048)
            nc.sync.dma_start(out=probs[:, c0 + lo : c0 + end], in_=e[:, 2 + skip + lo : 2 + skip + end])

        def finish(n):
            i = n % NT
            e = small[("e", n)]
            s = small[("s", n)]
            r = stats.tile([P, 1], F32, name="r")
            nc.vector.reciprocal(out=r[:], in_=s[:])
            if n < NT:
                nc.gpsimd.tensor_scalar(
                    out=head_last[:, i, :], in0=e[:, V : V + 8], scalar1=r[:, 0:1], scalar2=0.0,
                    op0=ALU.mult, op1=ALU.add,
                )
                steps = ((0, 1032, 0, 1024), (1032, 2046, 1024, 2040))
                for c0, c1, lo, hi in steps:
                    nc.gpsimd.tensor_scalar(
                        out=e[:, 8 + c0 : 8 + c1], in0=e[:, 8 + c0 : 8 + c1],
                        scalar1=r[:, 0:1], scalar2=0.0, op0=ALU.mult, op1=ALU.add,
                    )
                    store_head(e, i, lo, hi)
                if i % 4 > 0:
                    nc.gpsimd.tensor_copy(out=head_first[:, i, 0:6], in_=e[:, 8:14])
            else:
                cluster = head_last[:, i, 6:7]
                if n < 2 * NT - 1:
                    engine = nc.vector if n == 2 * NT - 2 else nc.gpsimd
                    cuts = (0, 1024, V) if n < 2 * NT - 2 else (0, V)
                    for lo, hi in zip(cuts[:-1], cuts[1:]):
                        engine.tensor_scalar(
                            out=e[:, 8 + lo : 8 + hi], in0=e[:, 8 + lo : 8 + hi],
                            scalar1=r[:, 0:1], scalar2=cluster, op0=ALU.mult, op1=ALU.mult,
                        )
                        store_tail(e, i, lo, hi if hi < V else 2056)
                else:
                    rc = stats.tile([P, 1], F32, name="rc")
                    nc.vector.tensor_scalar(
                        out=rc[:], in0=r[:], scalar1=cluster, scalar2=None, op0=ALU.mult
                    )
                    nc.vector.tensor_scalar(
                        out=e[:, 8 : 8 + LAST_SPLIT], in0=e[:, 8 : 8 + LAST_SPLIT],
                        scalar1=rc[:, 0:1], scalar2=None, op0=ALU.mult,
                    )
                    nc.scalar.activation(
                        out=e[:, 8 + LAST_SPLIT : 8 + V], in_=e[:, 8 + LAST_SPLIT : 8 + V], func=ACT.Copy,
                        scale=rc[:, 0:1],
                    )
                    store_tail(e, i, 0, LAST_SPLIT)
                    store_tail(e, i, LAST_SPLIT)

        first = ("A0", "A1", "B0", "B1", "B2", "B3", "B4", "B5", "B6", "B7")
        for k, u in enumerate(first):
            regroup(u)
            if k >= 1:
                quantise(first[k - 1])
            if k == 2:
                for i in range(2):
                    x_transpose(i)
                    x_out(i)
            if k == 3:
                for i in range(2):
                    x_quantise(i)
            if k == 9:
                for i in range(2, 4):
                    x_transpose(i)
                    x_out(i)
        for u in first[-1:]:
            quantise(u)
        logits(0)
        for i in range(4, NT):
            x_transpose(i)
            x_out(i)
        row_max(0)
        negate_max(0)
        for i in range(2, 4):
            x_quantise(i)
        for u in ('C0',):
            regroup(u)

        h_tiles = {2: (0, 1), 4: (2, 3), 5: (4, 5), 6: (6, 7)}
        late_units = {0: ('C1',), 1: ('C2',), 3: ('C3',)}
        late_quantises = {0: ('C0',), 1: ('C1',), 2: ('C2',), 4: ('C3',)}
        for n in range(2 * NT):
            exps(n)
            if n + 1 < 2 * NT:
                logits(n + 1)
            for u in late_units.get(n, ()):
                if u in BY_SCALAR:
                    regroup(u)
            for i in h_tiles.get(n, ()):
                h_matmuls(i)
            for i in h_tiles.get(n, ()):
                h_out(i)
            if n + 1 < 2 * NT:
                row_max(n + 1, range(2))
            if n > 0:
                finish(n - 1)
            if n + 1 < 2 * NT:
                row_max(n + 1, range(2, 4))
                negate_max(n + 1)
            if n == 0:
                for i in range(4, NT):
                    x_quantise(i)
            for u in late_quantises.get(n, ()):
                quantise(u)
            if n == 5:
                h_quantise(0)
            if n == 7:
                h_quantise(1)
            for u in late_units.get(n, ()):
                if u not in BY_SCALAR:
                    regroup(u)
            if n == 10:
                other = keep.tile([P, NT], F32)
                nc.scalar.copy(out=other[:], in_=head_last[:, :, 7])
                nc.sync.dma_start(out=o1.rearrange("(p i) o -> p (i o)", i=NT), in_=other[:])
        finish(2 * NT - 1)
